import numpy as np
import ml_dtypes


def mxq(x, axis, fmt="e4m3"):
    dtype, down = {"e4m3": (ml_dtypes.float8_e4m3fn, 7), "e5m2": (ml_dtypes.float8_e5m2, 14)}[fmt]
    v = np.moveaxis(np.asarray(x, np.float32).astype(ml_dtypes.bfloat16).astype(np.float64), axis, -1)
    blocks = v.reshape(v.shape[:-1] + (-1, 32))
    amax = np.abs(blocks).max(-1, keepdims=True)
    byte = np.maximum(np.where(amax > 0, np.frexp(amax)[1] - 1 + 127, 0) - down, 1)
    scale = np.exp2(byte - 127.0)
    codes = (blocks / scale).astype(np.float32).astype(dtype).astype(np.float64)
    return np.moveaxis((codes * scale).reshape(v.shape), -1, axis)


WIDE = False


def mx_kscale(k):
    if not WIDE:
        return np.ones(k)
    levels = np.array([10, -10, 5, -5, 0])
    a = np.random.permutation(np.resize(levels, k // 512 * 4)).reshape(k // 512, 4)
    idx = np.arange(k)
    return np.exp2(a[idx // 512, idx % 128 // 32])


BF16 = ml_dtypes.bfloat16


def bf(x):
    return np.asarray(x, np.float32).astype(BF16)


def f64(x):
    return np.asarray(x).astype(np.float64)


BATCH, OUTPUT_R, KERNEL, INPUT_DEPTH, OUTPUT_DEPTH, SIX = 8192, 1, 8, 16, 64, 6
INPUT_R = OUTPUT_R * KERNEL
P = OUTPUT_R ** 2
G = OUTPUT_DEPTH * SIX
W = KERNEL ** 2 * INPUT_DEPTH
ROWS = P * G
COLS = INPUT_R ** 2 * INPUT_DEPTH
IDX = np.arange(COLS).reshape(OUTPUT_R, KERNEL, OUTPUT_R, KERNEL * INPUT_DEPTH).transpose(0, 2, 1, 3).reshape(P, W)


def setup_inputs():
    s = mx_kscale(W)
    sc = np.empty(COLS)
    sc[IDX] = s
    c = np.mean(1.0 / s)
    window = np.zeros((P, COLS))
    window[np.arange(P)[:, None], IDX] = 1.0
    return {"x": bf(np.random.standard_normal((BATCH, COLS)) * 0.2 * np.sqrt(W) * c * sc),
            "connect_w": bf(np.random.standard_normal((ROWS, COLS))),
            "connect_mask": bf(np.random.uniform(0.5, 1.5, (ROWS, COLS)) * np.repeat(window, G, axis=0) / sc)}


def reference(x, connect_w, connect_mask):
    w = np.exp(f64(connect_w)) * f64(connect_mask)
    w = w / np.sum(w, axis=-1, keepdims=True)
    xw = f64(x)[:, IDX].transpose(1, 0, 2)
    ww = np.take_along_axis(w.reshape(P, G, COLS), IDX[:, None, :], axis=2)
    out = mxq(xw, 2, "e4m3") @ mxq(ww, 2, "e4m3").transpose(0, 2, 1)
    return out.transpose(1, 0, 2).reshape(BATCH, -1, SIX)

@@ -1,0 +1,244 @@
+from contextlib import ExitStack
+
+import concourse.mybir as mybir
+from concourse.masks import make_identity
+
+F32 = mybir.dt.float32
+BF16 = mybir.dt.bfloat16
+U32 = mybir.dt.uint32
+U8 = mybir.dt.uint8
+FP8X4 = mybir.dt.float8_e4m3fn_x4
+ALU = mybir.AluOpType
+ACT = mybir.ActivationFunctionType
+AX = mybir.AxisListType
+
+P = 128
+BATCH = 8192
+K = 1024
+G = 384
+WT = G // P
+UT = 4
+UNITS = BATCH // (P * UT)
+BIG_BUFS = 18
+
+FLOPS = 2 * BATCH * K * G
+
+
+def tile_connectlayer_t_kernel(tc, x, connect_w, connect_mask, out):
+    nc = tc.nc
+    out2 = out.rearrange("b d s -> b (d s)")
+    with ExitStack() as ctx:
+        const = ctx.enter_context(tc.tile_pool(name="const", bufs=1))
+        wpool = ctx.enter_context(tc.tile_pool(name="wpool", bufs=1))
+        big = ctx.enter_context(tc.tile_pool(name="big", bufs=BIG_BUFS))
+        grp = ctx.enter_context(tc.tile_pool(name="grp", bufs=3))
+        cod = ctx.enter_context(tc.tile_pool(name="cod", bufs=3))
+        tp = ctx.enter_context(tc.psum_pool(name="tp", bufs=5))
+        oa = ctx.enter_context(tc.psum_pool(name="oa", bufs=2))
+        ob = ctx.enter_context(tc.psum_pool(name="ob", bufs=1))
+        ctx.enter_context(tc.manual_schedule())
+
+        ident_f = const.tile([P, P], F32, name="ident_f")
+        ident_b = const.tile([P, P], BF16, name="ident_b")
+        make_identity(nc, ident_b[:])
+        make_identity(nc, ident_f[:])
+        warm = const.tile([P, 2], F32, name="warm")
+        nc.vector.memset(warm[:, 0:1], 0.0)
+        nc.scalar.activation(out=warm[:, 1:2], in_=warm[:, 0:1], func=ACT.Exp)
+
+        cw = [wpool.tile([P, K], BF16, name="cw%d" % j) for j in range(WT)]
+        mk = wpool.tile([P, WT * K], BF16, name="mk")
+        for j in range(WT):
+            nc.sync.dma_start(out=cw[j][:], in_=connect_w[j * P : (j + 1) * P, :])
+        nc.sync.dma_start(
+            out=mk[:].rearrange("p (j k) -> p j k", j=WT),
+            in_=connect_mask.rearrange("(j p) k -> p j k", p=P),
+        )
+        xs = []
+        for i in range(UNITS):
+            xt = big.tile([P, UT * K], BF16, name="xs%d" % i, tag="big")
+            r0 = i * P * UT
+            nc.sync.dma_start(
+                out=xt[:], in_=x[r0 : r0 + P * UT, :].rearrange("(p t) k -> p (t k)", t=UT)
+            )
+            xs.append(xt)
+
+        nmax = wpool.tile([P, WT], F32, name="nmax")
+        rsum = wpool.tile([P, WT], F32, name="rsum")
+        rinv = wpool.tile([P, WT], F32, name="rinv")
+        ew = [wpool.tile([P, K], F32, name="ew%d" % j) for j in range(WT)]
+        wb = [wpool.tile([P, K], BF16, name="wb%d" % j) for j in range(WT)]
+        gw = wpool.tile([P, 2 * G * 4], BF16, name="gw", align_bytes=64)
+        wcod = wpool.tile([P, 2 * G], U32, name="wcod", align_bytes=64)
+        wsca = wpool.tile([P, 2 * G], U8, name="wsca", align_bytes=64)
+        for j in range(WT):
+            nc.vector.tensor_reduce(
+                out=nmax[:, j : j + 1], in_=cw[j][:], axis=AX.X, op=ALU.max, negate=True
+            )
+        for j in range(WT):
+            nc.scalar.activation(
+                out=ew[j][:], in_=cw[j][:], func=ACT.Exp, bias=nmax[:, j : j + 1], scale=1.0
+            )
+        for j in range(WT):
+            nc.vector.scalar_tensor_tensor(
+                out=ew[j][:],
+                in0=ew[j][:],
+                scalar=1.0,
+                in1=mk[:, j * K : (j + 1) * K],
+                op0=ALU.mult,
+                op1=ALU.mult,
+                accum_out=rsum[:, j : j + 1],
+            )
+            nc.vector.reciprocal(out=rinv[:, j : j + 1], in_=rsum[:, j : j + 1])
+            nc.scalar.activation(
+                out=wb[j][:].rearrange("p (a e q) -> p a e q", a=4, e=2, q=P),
+                in_=ew[j][:].rearrange("p (a q e) -> p a e q", a=4, q=P, e=2),
+                func=ACT.Copy,
+                scale=rinv[:, j : j + 1],
+            )
+
+        banks = {}
+        halves = {}
+        codes = {}
+        outs = {}
+
+        def transposes(i, t):
+            bank = tp.tile([P, 512], F32, name="tp_%d_%d" % (i, t), tag="tp")
+            xw = xs[i][:].bitcast(F32)
+            for s in range(4):
+                nc.tensor.transpose(
+                    bank[:, s * P : (s + 1) * P],
+                    xw[:, t * 512 + s * P : t * 512 + (s + 1) * P],
+                    ident_f[:],
+                )
+            banks[(i, t)] = bank
+
+        def regroup(eng_copy, i, t):
+            h = t // 2
+            if (i, h) not in halves:
+                halves[(i, h)] = grp.tile(
+                    [P, 2048], BF16, name="g%d_%d" % (i, h), tag="g%d" % h, align_bytes=64
+                )
+            dst = halves[(i, h)][:].bitcast(F32)[:, (t % 2) * 512 : (t % 2 + 1) * 512]
+            eng_copy(
+                out=dst.rearrange("p (g b u) -> p g b u", g=2, b=P, u=2),
+                in_=banks[(i, t)][:].rearrange("p (g u b) -> p g b u", g=2, u=2, b=P),
+            )
+
+        def quantise(i, h):
+            c = cod.tile([P, 512], U32, name="c%d_%d" % (i, h), tag="c%d" % h, align_bytes=64)
+            s = cod.tile([P, 512], U8, name="s%d_%d" % (i, h), tag="s%d" % h, align_bytes=64)
+            nc.vector.quantize_mx(out=c[:].bitcast(FP8X4), scales=s[:], in_=halves[(i, h)][:])
+            codes[(i, h)] = (c, s)
+
+        def mx_group(dst, i, t, c0, c1):
+            c, s = codes[(i, t // 2)]
+            for g in range(2):
+                a = ((t % 2) * 2 + g) * P
+                nc.tensor.matmul_mx(
+                    out=dst,
+                    lhsT=c[:, a : a + P].bitcast(FP8X4),
+                    lhsT_scale=s[:, a : a + P],
+                    rhs=wcod[:, g * G + c0 : g * G + c1].bitcast(FP8X4),
+                    rhs_scale=wsca[:, g * G + c0 : g * G + c1],
+                    start=(g == 0),
+                    stop=(g == 1),
+                )
+
+        def multiply(i):
+            acc = []
+            for h in range(2):
+                a = oa.tile([P, 512], F32, name="oa%d_%d" % (i, h), tag="oa")
+                for tt in range(2):
+                    mx_group(a[:, tt * 256 : (tt + 1) * 256], i, 2 * h + tt, 0, 256)
+                acc.append(a)
+            b = ob.tile([P, 512], F32, name="ob%d" % i, tag="ob")
+            for t in range(UT):
+                mx_group(b[:, t * P : (t + 1) * P], i, t, 256, G)
+            acc.append(b)
+            outs[i] = (acc, big.tile([P, UT * G], F32, name="os%d" % i, tag="big"))
+
+        def drain_a(i, h):
+            acc, o = outs[i]
+            nc.scalar.copy(
+                out=o[:].rearrange("p (t c) -> p t c", t=UT)[:, 2 * h : 2 * h + 2, 0:256],
+                in_=acc[h][:].rearrange("p (t c) -> p t c", t=2),
+            )
+
+        def drain_b_store(i):
+            acc, o = outs[i]
+            nc.vector.tensor_copy(
+                out=o[:].rearrange("p (t c) -> p t c", t=UT)[:, :, 256:G],
+                in_=acc[2][:].rearrange("p (t c) -> p t c", t=UT),
+            )
+            r0 = i * P * UT
+            nc.sync.dma_start(
+                out=out2[r0 : r0 + P * UT, :].rearrange("(p t) c -> p (t c)", t=UT), in_=o[:]
+            )
+
+        wbank = []
+
+        def w_transposes(j):
+            pool = oa if j < 2 else ob
+            b = pool.tile([P, K], BF16, name="wt%d" % j, tag="oa" if j < 2 else "ob")
+            for s in range(8):
+                nc.tensor.transpose(
+                    b[:, s * P : (s + 1) * P], wb[j][:, s * P : (s + 1) * P], ident_b[:]
+                )
+            wbank.append(b)
+
+        def w_regroup(eng_copy, j):
+            eng_copy(
+                out=gw[:].rearrange("p (g c t) -> p g c t", g=2, c=G, t=4)[
+                    :, :, j * P : (j + 1) * P, :
+                ],
+                in_=wbank[j][:].rearrange("p (g t c) -> p g c t", g=2, t=4, c=P),
+            )
+
+        def w_quantise(j):
+            for g in range(2):
+                a = g * G + j * P
+                nc.vector.quantize_mx(
+                    out=wcod[:, a : a + P].bitcast(FP8X4),
+                    scales=wsca[:, a : a + P],
+                    in_=gw[:, a * 4 : (a + P) * 4],
+                )
+
+        transposes(0, 0)
+        transposes(0, 1)
+        w_transposes(0)
+        w_transposes(1)
+        w_transposes(2)
+        transposes(0, 2)
+        transposes(0, 3)
+        regroup(nc.vector.tensor_copy, 0, 0)
+        regroup(nc.scalar.copy, 0, 1)
+        w_regroup(nc.vector.tensor_copy, 0)
+        w_regroup(nc.scalar.copy, 1)
+        w_quantise(0)
+        w_regroup(nc.vector.tensor_copy, 2)
+        regroup(nc.scalar.copy, 0, 2)
+        regroup(nc.scalar.copy, 0, 3)
+        w_quantise(1)
+        w_quantise(2)
+        quantise(0, 0)
+        quantise(0, 1)
+
+        for i in range(UNITS):
+            n = i + 1
+            if n < UNITS:
+                for t in range(UT):
+                    transposes(n, t)
+            if i >= 1:
+                drain_b_store(i - 1)
+            if n < UNITS:
+                regroup(nc.scalar.copy, n, 0)
+                regroup(nc.scalar.copy, n, 1)
+                regroup(nc.vector.tensor_copy, n, 2)
+                regroup(nc.scalar.copy, n, 3)
+                quantise(n, 0)
+                quantise(n, 1)
+            multiply(i)
+            drain_a(i, 0)
+            drain_a(i, 1)
+        drain_b_store(UNITS - 1)

@@ -17,9 +17,11 @@ BATCH = 8192
 K = 1024
 G = 384
 WT = G // P
-UT = 4
-UNITS = BATCH // (P * UT)
-BIG_BUFS = 18
+TILES = BATCH // P
+RUN = 4
+CHUNKS = (2, 2, 4, 8, 8, 8, 8, 8, 8, 8)
+OUT_BUFS = ((0, 4), (4, 4), (8, 8), (16, 8), (24, 8), (32, 8), (40, 8), (48, 8), (56, 4), (60, 4))
+STORES = ((0, 2), (2, 2), (4, 4), (8, 8), (16, 8), (24, 8), (32, 8), (40, 8), (48, 8), (56, 4), (60, 2), (62, 1), (63, 1))
 
 FLOPS = 2 * BATCH * K * G
 
@@ -30,9 +32,9 @@ def tile_connectlayer_t_kernel(tc, x, connect_w, connect_mask, out):
     with ExitStack() as ctx:
         const = ctx.enter_context(tc.tile_pool(name="const", bufs=1))
         wpool = ctx.enter_context(tc.tile_pool(name="wpool", bufs=1))
-        big = ctx.enter_context(tc.tile_pool(name="big", bufs=BIG_BUFS))
-        grp = ctx.enter_context(tc.tile_pool(name="grp", bufs=3))
-        cod = ctx.enter_context(tc.tile_pool(name="cod", bufs=3))
+        xo = ctx.enter_context(tc.tile_pool(name="xo", bufs=1))
+        grp = ctx.enter_context(tc.tile_pool(name="grp", bufs=4))
+        cod = ctx.enter_context(tc.tile_pool(name="cod", bufs=6))
         tp = ctx.enter_context(tc.psum_pool(name="tp", bufs=5))
         oa = ctx.enter_context(tc.psum_pool(name="oa", bufs=2))
         ob = ctx.enter_context(tc.psum_pool(name="ob", bufs=1))
@@ -40,28 +42,42 @@ def tile_connectlayer_t_kernel(tc, x, connect_w, connect_mask, out):
 
         ident_f = const.tile([P, P], F32, name="ident_f")
         ident_b = const.tile([P, P], BF16, name="ident_b")
-        make_identity(nc, ident_b[:])
         make_identity(nc, ident_f[:])
+        make_identity(nc, ident_b[:])
         warm = const.tile([P, 2], F32, name="warm")
         nc.vector.memset(warm[:, 0:1], 0.0)
         nc.scalar.activation(out=warm[:, 1:2], in_=warm[:, 0:1], func=ACT.Exp)
 
         cw = [wpool.tile([P, K], BF16, name="cw%d" % j) for j in range(WT)]
-        mk = wpool.tile([P, WT * K], BF16, name="mk")
-        for j in range(WT):
-            nc.sync.dma_start(out=cw[j][:], in_=connect_w[j * P : (j + 1) * P, :])
-        nc.sync.dma_start(
-            out=mk[:].rearrange("p (j k) -> p j k", j=WT),
-            in_=connect_mask.rearrange("(j p) k -> p j k", p=P),
-        )
-        xs = []
-        for i in range(UNITS):
-            xt = big.tile([P, UT * K], BF16, name="xs%d" % i, tag="big")
-            r0 = i * P * UT
+        mk = [wpool.tile([P, K], BF16, name="mk%d" % j) for j in range(WT)]
+        chunk_of = {}
+        chunk_tiles = []
+        first = 0
+        for n in CHUNKS:
+            xt = xo.tile([P, n * K], BF16, name="x%d" % first, offset=first * K * 2)
+            chunk_tiles.append((xt, first, n))
+            for t in range(n):
+                chunk_of[first + t] = (xt, first, n)
+            first += n
+
+        def load_w(dst, src, j):
+            nc.sync.dma_start(out=dst[j][:], in_=src[j * P : (j + 1) * P, :])
+
+        def load_x(c):
+            xt, f, n = chunk_tiles[c]
             nc.sync.dma_start(
-                out=xt[:], in_=x[r0 : r0 + P * UT, :].rearrange("(p t) k -> p (t k)", t=UT)
+                out=xt[:], in_=x[f * P : (f + n) * P, :].rearrange("(p t) k -> p (t k)", t=n)
             )
-            xs.append(xt)
+
+        for j in range(WT):
+            load_w(cw, connect_w, j)
+        load_x(0)
+        load_w(mk, connect_mask, 0)
+        load_x(1)
+        load_w(mk, connect_mask, 1)
+        load_w(mk, connect_mask, 2)
+        for c in range(2, len(CHUNKS)):
+            load_x(c)
 
         nmax = wpool.tile([P, WT], F32, name="nmax")
         rsum = wpool.tile([P, WT], F32, name="rsum")
@@ -84,7 +100,7 @@ def tile_connectlayer_t_kernel(tc, x, connect_w, connect_mask, out):
                 out=ew[j][:],
                 in0=ew[j][:],
                 scalar=1.0,
-                in1=mk[:, j * K : (j + 1) * K],
+                in1=mk[j][:],
                 op0=ALU.mult,
                 op1=ALU.mult,
                 accum_out=rsum[:, j : j + 1],
@@ -100,39 +116,38 @@ def tile_connectlayer_t_kernel(tc, x, connect_w, connect_mask, out):
         banks = {}
         halves = {}
         codes = {}
-        outs = {}
+        out_of = {}
+        state = {"pending": None, "store": 0}
+        drained = set()
 
-        def transposes(i, t):
-            bank = tp.tile([P, 512], F32, name="tp_%d_%d" % (i, t), tag="tp")
-            xw = xs[i][:].bitcast(F32)
+        def transposes(t):
+            xt, f, n = chunk_of[t]
+            bank = tp.tile([P, 512], F32, name="tp%d" % t, tag="tp")
+            xw = xt[:].bitcast(F32)
             for s in range(4):
-                nc.tensor.transpose(
-                    bank[:, s * P : (s + 1) * P],
-                    xw[:, t * 512 + s * P : t * 512 + (s + 1) * P],
-                    ident_f[:],
-                )
-            banks[(i, t)] = bank
+                a = (t - f) * 512 + s * P
+                nc.tensor.transpose(bank[:, s * P : (s + 1) * P], xw[:, a : a + P], ident_f[:])
+            banks[t] = bank
 
-        def regroup(eng_copy, i, t):
-            h = t // 2
-            if (i, h) not in halves:
-                halves[(i, h)] = grp.tile(
-                    [P, 2048], BF16, name="g%d_%d" % (i, h), tag="g%d" % h, align_bytes=64
-                )
-            dst = halves[(i, h)][:].bitcast(F32)[:, (t % 2) * 512 : (t % 2 + 1) * 512]
-            eng_copy(
+        def regroup(t, on_vector):
+            q = t // 2
+            if q not in halves:
+                halves[q] = grp.tile([P, 2048], BF16, name="g%d" % q, tag="g", align_bytes=64)
+            dst = halves[q][:].bitcast(F32)[:, (t % 2) * 512 : (t % 2 + 1) * 512]
+            copy = nc.vector.tensor_copy if on_vector else nc.scalar.copy
+            copy(
                 out=dst.rearrange("p (g b u) -> p g b u", g=2, b=P, u=2),
-                in_=banks[(i, t)][:].rearrange("p (g u b) -> p g b u", g=2, u=2, b=P),
+                in_=banks[t][:].rearrange("p (g u b) -> p g b u", g=2, u=2, b=P),
             )
 
-        def quantise(i, h):
-            c = cod.tile([P, 512], U32, name="c%d_%d" % (i, h), tag="c%d" % h, align_bytes=64)
-            s = cod.tile([P, 512], U8, name="s%d_%d" % (i, h), tag="s%d" % h, align_bytes=64)
-            nc.vector.quantize_mx(out=c[:].bitcast(FP8X4), scales=s[:], in_=halves[(i, h)][:])
-            codes[(i, h)] = (c, s)
+        def quantise(q):
+            c = cod.tile([P, 512], U32, name="c%d" % q, tag="c", align_bytes=64)
+            s = cod.tile([P, 512], U8, name="s%d" % q, tag="s", align_bytes=64)
+            nc.vector.quantize_mx(out=c[:].bitcast(FP8X4), scales=s[:], in_=halves[q][:])
+            codes[q] = (c, s)
 
-        def mx_group(dst, i, t, c0, c1):
-            c, s = codes[(i, t // 2)]
+        def mx_group(dst, t, c0, c1):
+            c, s = codes[t // 2]
             for g in range(2):
                 a = ((t % 2) * 2 + g) * P
                 nc.tensor.matmul_mx(
@@ -145,36 +160,68 @@ def tile_connectlayer_t_kernel(tc, x, connect_w, connect_mask, out):
                     stop=(g == 1),
                 )
 
-        def multiply(i):
-            acc = []
-            for h in range(2):
-                a = oa.tile([P, 512], F32, name="oa%d_%d" % (i, h), tag="oa")
-                for tt in range(2):
-                    mx_group(a[:, tt * 256 : (tt + 1) * 256], i, 2 * h + tt, 0, 256)
-                acc.append(a)
-            b = ob.tile([P, 512], F32, name="ob%d" % i, tag="ob")
-            for t in range(UT):
-                mx_group(b[:, t * P : (t + 1) * P], i, t, 256, G)
-            acc.append(b)
-            outs[i] = (acc, big.tile([P, UT * G], F32, name="os%d" % i, tag="big"))
+        def out_view(t, n):
+            if t not in out_of:
+                for f, m in OUT_BUFS:
+                    if f <= t < f + m:
+                        o = xo.tile([P, m * G], F32, name="o%d" % f, offset=f * G * 4)
+                        for k in range(m):
+                            out_of[f + k] = (o, f, m)
+            o, f, m = out_of[t]
+            return o[:].rearrange("p (t c) -> p t c", t=m)[:, t - f : t - f + n, :]
 
-        def drain_a(i, h):
-            acc, o = outs[i]
-            nc.scalar.copy(
-                out=o[:].rearrange("p (t c) -> p t c", t=UT)[:, 2 * h : 2 * h + 2, 0:256],
-                in_=acc[h][:].rearrange("p (t c) -> p t c", t=2),
-            )
+        def stores():
+            while state["store"] < len(STORES):
+                t, n = STORES[state["store"]]
+                if not all((t + k, part) in drained for k in range(n) for part in "ab"):
+                    break
+                xt, f, m = chunk_of[t]
+                nc.sync.dma_start(
+                    out=out2[f * P : (f + m) * P, :].rearrange("(p t) c -> p t c", t=m)[
+                        :, t - f : t - f + n, :
+                    ],
+                    in_=out_view(t, n),
+                )
+                state["store"] += 1
 
-        def drain_b_store(i):
-            acc, o = outs[i]
-            nc.vector.tensor_copy(
-                out=o[:].rearrange("p (t c) -> p t c", t=UT)[:, :, 256:G],
-                in_=acc[2][:].rearrange("p (t c) -> p t c", t=UT),
-            )
-            r0 = i * P * UT
-            nc.sync.dma_start(
-                out=out2[r0 : r0 + P * UT, :].rearrange("(p t) c -> p (t c)", t=UT), in_=o[:]
-            )
+        def drain(acc, t, n, c0, c1, on_vector):
+            copy = nc.vector.tensor_copy if on_vector else nc.scalar.copy
+            copy(out=out_view(t, n)[:, :, c0:c1], in_=acc.rearrange("p (t c) -> p t c", t=n))
+            for k in range(n):
+                drained.add((t + k, "a" if c0 == 0 else "b"))
+
+        def flush_b():
+            if state["pending"] is not None:
+                acc, t = state["pending"]
+                drain(acc[:], t, 4, 256, G, True)
+                state["pending"] = None
+                stores()
+
+        def m_run(first_tile, count):
+            for t in range(first_tile, first_tile + count, 4):
+                flush_b()
+                accs = []
+                for h in range(2):
+                    a = oa.tile([P, 512], F32, name="oa%d" % (t + 2 * h), tag="oa")
+                    for k in range(2):
+                        mx_group(a[:, k * 256 : (k + 1) * 256], t + 2 * h + k, 0, 256)
+                    accs.append(a)
+                b = ob.tile([P, 512], F32, name="ob%d" % t, tag="ob")
+                for k in range(4):
+                    mx_group(b[:, k * P : (k + 1) * P], t + k, 256, G)
+                for h in range(2):
+                    drain(accs[h][:], t + 2 * h, 2, 0, 256, False)
+                state["pending"] = (b, t)
+
+        def t_run(first_tile, count, vector_tiles):
+            for k in range(count):
+                transposes(first_tile + k)
+                if k == 0:
+                    flush_b()
+                regroup(first_tile + k, k in vector_tiles)
+                if k % 2 == 1 and k >= 3:
+                    quantise((first_tile + k - 3) // 2)
+            quantise((first_tile + count - 2) // 2)
 
         wbank = []
 
@@ -187,8 +234,9 @@ def tile_connectlayer_t_kernel(tc, x, connect_w, connect_mask, out):
                 )
             wbank.append(b)
 
-        def w_regroup(eng_copy, j):
-            eng_copy(
+        def w_regroup(j, on_vector):
+            copy = nc.vector.tensor_copy if on_vector else nc.scalar.copy
+            copy(
                 out=gw[:].rearrange("p (g c t) -> p g c t", g=2, c=G, t=4)[
                     :, :, j * P : (j + 1) * P, :
                 ],
@@ -204,41 +252,58 @@ def tile_connectlayer_t_kernel(tc, x, connect_w, connect_mask, out):
                     in_=gw[:, a * 4 : (a + P) * 4],
                 )
 
-        transposes(0, 0)
-        transposes(0, 1)
-        w_transposes(0)
-        w_transposes(1)
-        w_transposes(2)
-        transposes(0, 2)
-        transposes(0, 3)
-        regroup(nc.vector.tensor_copy, 0, 0)
-        regroup(nc.scalar.copy, 0, 1)
-        w_regroup(nc.vector.tensor_copy, 0)
-        w_regroup(nc.scalar.copy, 1)
+        for t in range(4):
+            transposes(t)
+        for j in range(WT):
+            w_transposes(j)
+        regroup(0, True)
+        regroup(1, True)
+        w_regroup(0, True)
+        w_regroup(1, False)
+        quantise(0)
         w_quantise(0)
-        w_regroup(nc.vector.tensor_copy, 2)
-        regroup(nc.scalar.copy, 0, 2)
-        regroup(nc.scalar.copy, 0, 3)
         w_quantise(1)
+        regroup(2, False)
+        regroup(3, False)
+        w_regroup(2, False)
+        quantise(1)
         w_quantise(2)
-        quantise(0, 0)
-        quantise(0, 1)
+        transposes(4)
+        regroup(4, False)
+        transposes(5)
+        regroup(5, False)
+        quantise(2)
 
-        for i in range(UNITS):
-            n = i + 1
-            if n < UNITS:
-                for t in range(UT):
-                    transposes(n, t)
-            if i >= 1:
-                drain_b_store(i - 1)
-            if n < UNITS:
-                regroup(nc.scalar.copy, n, 0)
-                regroup(nc.scalar.copy, n, 1)
-                regroup(nc.vector.tensor_copy, n, 2)
-                regroup(nc.scalar.copy, n, 3)
-                quantise(n, 0)
-                quantise(n, 1)
-            multiply(i)
-            drain_a(i, 0)
-            drain_a(i, 1)
-        drain_b_store(UNITS - 1)
+        m_run(0, 4)
+        t_run(6, 6, (2, 5))
+        m_run(4, 4)
+        if RUN == 4:
+            for a in range(12, TILES, 4):
+                t_run(a, 4, (2,))
+                m_run(a - 4, 4)
+        else:
+            for a in range(12, TILES - 4, 8):
+                t_run(a, 8, (2, 5, 7))
+                m_run(a - 4, 8)
+            t_run(TILES - 4, 4, (2,))
+            m_run(TILES - 8, 4)
+
+        flush_b()
+        t = TILES - 4
+        b = tp.tile([P, 512], F32, name="last_b", tag="tp")
+        for k in range(4):
+            mx_group(b[:, k * P : (k + 1) * P], t + k, 256, G)
+        drain(b[:], t, 4, 256, G, True)
+        a = oa.tile([P, 512], F32, name="last_a", tag="oa")
+        for k in range(2):
+            mx_group(a[:, k * 256 : (k + 1) * 256], t + k, 0, 256)
+        drain(a[:], t, 2, 0, 256, False)
+        stores()
+        a2 = oa.tile([P, 256], F32, name="last_a2", tag="oa")
+        mx_group(a2[:], t + 2, 0, 256)
+        drain(a2[:], t + 2, 1, 0, 256, False)
+        stores()
+        a3 = tp.tile([P, 256], F32, name="last_a3", tag="tp")
+        mx_group(a3[:], t + 3, 0, 256)
+        drain(a3[:], t + 3, 1, 0, 256, True)
+        stores()

@@ -18,8 +18,8 @@ K = 1024
 G = 384
 WT = G // P
 TILES = BATCH // P
-RUN = 4
-CHUNKS = (2, 2, 4, 8, 8, 8, 8, 8, 8, 8)
+RUN = 8
+CHUNKS = (2, 2, 4, 8, 8, 8, 16, 16)
 OUT_BUFS = ((0, 4), (4, 4), (8, 8), (16, 8), (24, 8), (32, 8), (40, 8), (48, 8), (56, 4), (60, 4))
 STORES = ((0, 2), (2, 2), (4, 4), (8, 8), (16, 8), (24, 8), (32, 8), (40, 8), (48, 8), (56, 4), (60, 2), (62, 1), (63, 1))
 
@@ -33,8 +33,8 @@ def tile_connectlayer_t_kernel(tc, x, connect_w, connect_mask, out):
         const = ctx.enter_context(tc.tile_pool(name="const", bufs=1))
         wpool = ctx.enter_context(tc.tile_pool(name="wpool", bufs=1))
         xo = ctx.enter_context(tc.tile_pool(name="xo", bufs=1))
-        grp = ctx.enter_context(tc.tile_pool(name="grp", bufs=4))
-        cod = ctx.enter_context(tc.tile_pool(name="cod", bufs=6))
+        grp = ctx.enter_context(tc.tile_pool(name="grp", bufs=6))
+        cod = ctx.enter_context(tc.tile_pool(name="cod", bufs=10))
         tp = ctx.enter_context(tc.psum_pool(name="tp", bufs=5))
         oa = ctx.enter_context(tc.psum_pool(name="oa", bufs=2))
         ob = ctx.enter_context(tc.psum_pool(name="ob", bufs=1))

@@ -18,28 +18,32 @@ K = 1024
 G = 384
 WT = G // P
 TILES = BATCH // P
-RUN = 8
-CHUNKS = (2, 2, 4, 8, 8, 8, 16, 16)
-OUT_BUFS = ((0, 4), (4, 4), (8, 8), (16, 8), (24, 8), (32, 8), (40, 8), (48, 8), (56, 4), (60, 4))
-STORES = ((0, 2), (2, 2), (4, 4), (8, 8), (16, 8), (24, 8), (32, 8), (40, 8), (48, 8), (56, 4), (60, 2), (62, 1), (63, 1))
+X_BASE = 16384
+LOADS = (2, 2, 4, 8, 8, 8, 16, 16)
+OUT_BUFS = ((0, 16), (16, 16), (32, 8), (40, 8), (48, 8), (56, 4), (60, 4))
+STORES = ((0, 16), (16, 16), (32, 8), (40, 8), (48, 8), (56, 4), (60, 2), (62, 1), (63, 1))
 
 FLOPS = 2 * BATCH * K * G
 
 
 def tile_connectlayer_t_kernel(tc, x, connect_w, connect_mask, out):
     nc = tc.nc
-    out2 = out.rearrange("b d s -> b (d s)")
+    x3 = x.rearrange("(p t) k -> p t k", t=TILES)
+    out3 = out.rearrange("(p t) d s -> p t (d s)", t=TILES)
     with ExitStack() as ctx:
         const = ctx.enter_context(tc.tile_pool(name="const", bufs=1))
         wpool = ctx.enter_context(tc.tile_pool(name="wpool", bufs=1))
         xo = ctx.enter_context(tc.tile_pool(name="xo", bufs=1))
-        grp = ctx.enter_context(tc.tile_pool(name="grp", bufs=6))
-        cod = ctx.enter_context(tc.tile_pool(name="cod", bufs=10))
-        tp = ctx.enter_context(tc.psum_pool(name="tp", bufs=5))
+        grp = ctx.enter_context(tc.tile_pool(name="grp", bufs=4))
+        cod = ctx.enter_context(tc.tile_pool(name="cod", bufs=6))
+        tp = ctx.enter_context(tc.psum_pool(name="tp", bufs=4))
         oa = ctx.enter_context(tc.psum_pool(name="oa", bufs=2))
         ob = ctx.enter_context(tc.psum_pool(name="ob", bufs=1))
+        ex = ctx.enter_context(tc.psum_pool(name="ex", bufs=1))
         ctx.enter_context(tc.manual_schedule())
 
+        zeros = const.tile([P, 512], BF16, name="zeros")
+        nc.vector.memset(zeros[:], 0.0)
         ident_f = const.tile([P, P], F32, name="ident_f")
         ident_b = const.tile([P, P], BF16, name="ident_b")
         make_identity(nc, ident_f[:])
@@ -53,11 +57,11 @@ def tile_connectlayer_t_kernel(tc, x, connect_w, connect_mask, out):
         chunk_of = {}
         chunk_tiles = []
         first = 0
-        for n in CHUNKS:
-            xt = xo.tile([P, n * K], BF16, name="x%d" % first, offset=first * K * 2)
+        for n in LOADS:
+            xt = xo.tile([P, n * K], BF16, name="x%d" % first, offset=X_BASE + first * K * 2)
             chunk_tiles.append((xt, first, n))
             for t in range(n):
-                chunk_of[first + t] = (xt, first, n)
+                chunk_of[first + t] = (xt, first)
             first += n
 
         def load_w(dst, src, j):
@@ -66,7 +70,7 @@ def tile_connectlayer_t_kernel(tc, x, connect_w, connect_mask, out):
         def load_x(c):
             xt, f, n = chunk_tiles[c]
             nc.sync.dma_start(
-                out=xt[:], in_=x[f * P : (f + n) * P, :].rearrange("(p t) k -> p (t k)", t=n)
+                out=xt[:].rearrange("p (t k) -> p t k", t=n), in_=x3[:, f : f + n, :]
             )
 
         for j in range(WT):
@@ -76,7 +80,7 @@ def tile_connectlayer_t_kernel(tc, x, connect_w, connect_mask, out):
         load_x(1)
         load_w(mk, connect_mask, 1)
         load_w(mk, connect_mask, 2)
-        for c in range(2, len(CHUNKS)):
+        for c in range(2, len(LOADS)):
             load_x(c)
 
         nmax = wpool.tile([P, WT], F32, name="nmax")
@@ -121,7 +125,7 @@ def tile_connectlayer_t_kernel(tc, x, connect_w, connect_mask, out):
         drained = set()
 
         def transposes(t):
-            xt, f, n = chunk_of[t]
+            xt, f = chunk_of[t]
             bank = tp.tile([P, 512], F32, name="tp%d" % t, tag="tp")
             xw = xt[:].bitcast(F32)
             for s in range(4):
@@ -175,13 +179,7 @@ def tile_connectlayer_t_kernel(tc, x, connect_w, connect_mask, out):
                 t, n = STORES[state["store"]]
                 if not all((t + k, part) in drained for k in range(n) for part in "ab"):
                     break
-                xt, f, m = chunk_of[t]
-                nc.sync.dma_start(
-                    out=out2[f * P : (f + m) * P, :].rearrange("(p t) c -> p t c", t=m)[
-                        :, t - f : t - f + n, :
-                    ],
-                    in_=out_view(t, n),
-                )
+                nc.sync.dma_start(out=out3[:, t : t + n, :], in_=out_view(t, n))
                 state["store"] += 1
 
         def drain(acc, t, n, c0, c1, on_vector):
@@ -197,33 +195,39 @@ def tile_connectlayer_t_kernel(tc, x, connect_w, connect_mask, out):
                 state["pending"] = None
                 stores()
 
-        def m_run(first_tile, count):
-            for t in range(first_tile, first_tile + count, 4):
-                flush_b()
-                accs = []
-                for h in range(2):
-                    a = oa.tile([P, 512], F32, name="oa%d" % (t + 2 * h), tag="oa")
-                    for k in range(2):
-                        mx_group(a[:, k * 256 : (k + 1) * 256], t + 2 * h + k, 0, 256)
-                    accs.append(a)
+        def m_run(t):
+            flush_b()
+            accs = []
+            for h in range(2):
+                a = oa.tile([P, 512], F32, name="oa%d" % (t + 2 * h), tag="oa")
+                for k in range(2):
+                    mx_group(a[:, k * 256 : (k + 1) * 256], t + 2 * h + k, 0, 256)
+                accs.append(a)
+            if (t // 4) % 2 == 0:
                 b = ob.tile([P, 512], F32, name="ob%d" % t, tag="ob")
-                for k in range(4):
-                    mx_group(b[:, k * P : (k + 1) * P], t + k, 256, G)
-                for h in range(2):
-                    drain(accs[h][:], t + 2 * h, 2, 0, 256, False)
-                state["pending"] = (b, t)
+            else:
+                b = ex.tile([P, 512], F32, name="ex%d" % t, tag="ex")
+            for k in range(4):
+                mx_group(b[:, k * P : (k + 1) * P], t + k, 256, G)
+            for h in range(2):
+                drain(accs[h][:], t + 2 * h, 2, 0, 256, False)
+            state["pending"] = (b, t)
 
-        def t_run(first_tile, count, vector_tiles):
-            for k in range(count):
+        def t_run(first_tile):
+            for k in range(4):
                 transposes(first_tile + k)
                 if k == 0:
                     flush_b()
-                regroup(first_tile + k, k in vector_tiles)
-                if k % 2 == 1 and k >= 3:
-                    quantise((first_tile + k - 3) // 2)
-            quantise((first_tile + count - 2) // 2)
+                regroup(first_tile + k, k == 2)
+            quantise(first_tile // 2)
+            quantise(first_tile // 2 + 1)
 
         wbank = []
+        junk = ex.tile([P, 512], F32, name="junk", tag="ex")
+
+        def idle_matmuls(n):
+            for i in range(n):
+                nc.tensor.matmul(out=junk[:], lhsT=zeros[:, 0:P], rhs=zeros[:], start=True, stop=True)
 
         def w_transposes(j):
             pool = oa if j < 2 else ob
@@ -252,10 +256,19 @@ def tile_connectlayer_t_kernel(tc, x, connect_w, connect_mask, out):
                     in_=gw[:, a * 4 : (a + P) * 4],
                 )
 
-        for t in range(4):
-            transposes(t)
-        for j in range(WT):
-            w_transposes(j)
+        idle_matmuls(10)
+        transposes(0)
+        transposes(1)
+        idle_matmuls(2)
+        transposes(2)
+        transposes(3)
+        idle_matmuls(3)
+        w_transposes(0)
+        idle_matmuls(2)
+        w_transposes(1)
+        idle_matmuls(2)
+        w_transposes(2)
+        idle_matmuls(2)
         regroup(0, True)
         regroup(1, True)
         w_regroup(0, True)
@@ -272,21 +285,19 @@ def tile_connectlayer_t_kernel(tc, x, connect_w, connect_mask, out):
         regroup(4, False)
         transposes(5)
         regroup(5, False)
+        idle_matmuls(2)
         quantise(2)
+        transposes(6)
+        regroup(6, False)
+        transposes(7)
+        regroup(7, True)
+        idle_matmuls(2)
+        quantise(3)
 
-        m_run(0, 4)
-        t_run(6, 6, (2, 5))
-        m_run(4, 4)
-        if RUN == 4:
-            for a in range(12, TILES, 4):
-                t_run(a, 4, (2,))
-                m_run(a - 4, 4)
-        else:
-            for a in range(12, TILES - 4, 8):
-                t_run(a, 8, (2, 5, 7))
-                m_run(a - 4, 8)
-            t_run(TILES - 4, 4, (2,))
-            m_run(TILES - 8, 4)
+        m_run(0)
+        for a in range(8, TILES, 4):
+            t_run(a)
+            m_run(a - 4)
 
         flush_b()
         t = TILES - 4

@@ -10,7 +10,6 @@ U8 = mybir.dt.uint8
 FP8X4 = mybir.dt.float8_e4m3fn_x4
 ALU = mybir.AluOpType
 ACT = mybir.ActivationFunctionType
-AX = mybir.AxisListType
 
 P = 128
 BATCH = 8192
@@ -18,32 +17,28 @@ K = 1024
 G = 384
 WT = G // P
 TILES = BATCH // P
-X_BASE = 16384
-LOADS = (2, 2, 4, 8, 8, 8, 16, 16)
-OUT_BUFS = ((0, 16), (16, 16), (32, 8), (40, 8), (48, 8), (56, 4), (60, 4))
-STORES = ((0, 16), (16, 16), (32, 8), (40, 8), (48, 8), (56, 4), (60, 2), (62, 1), (63, 1))
+RUN = 4
+CHUNKS = (2, 2, 4, 8, 8, 8, 8, 8, 8, 8)
+OUT_BUFS = ((0, 4), (4, 4), (8, 8), (16, 8), (24, 8), (32, 8), (40, 8), (48, 8), (56, 4), (60, 4))
+STORES = ((0, 2), (2, 2), (4, 4), (8, 8), (16, 8), (24, 8), (32, 8), (40, 8), (48, 8), (56, 4), (60, 2), (62, 1), (63, 1))
 
 FLOPS = 2 * BATCH * K * G
 
 
 def tile_connectlayer_t_kernel(tc, x, connect_w, connect_mask, out):
     nc = tc.nc
-    x3 = x.rearrange("(p t) k -> p t k", t=TILES)
-    out3 = out.rearrange("(p t) d s -> p t (d s)", t=TILES)
+    out2 = out.rearrange("b d s -> b (d s)")
     with ExitStack() as ctx:
         const = ctx.enter_context(tc.tile_pool(name="const", bufs=1))
         wpool = ctx.enter_context(tc.tile_pool(name="wpool", bufs=1))
         xo = ctx.enter_context(tc.tile_pool(name="xo", bufs=1))
         grp = ctx.enter_context(tc.tile_pool(name="grp", bufs=4))
         cod = ctx.enter_context(tc.tile_pool(name="cod", bufs=6))
-        tp = ctx.enter_context(tc.psum_pool(name="tp", bufs=4))
+        tp = ctx.enter_context(tc.psum_pool(name="tp", bufs=5))
         oa = ctx.enter_context(tc.psum_pool(name="oa", bufs=2))
         ob = ctx.enter_context(tc.psum_pool(name="ob", bufs=1))
-        ex = ctx.enter_context(tc.psum_pool(name="ex", bufs=1))
         ctx.enter_context(tc.manual_schedule())
 
-        zeros = const.tile([P, 512], BF16, name="zeros")
-        nc.vector.memset(zeros[:], 0.0)
         ident_f = const.tile([P, P], F32, name="ident_f")
         ident_b = const.tile([P, P], BF16, name="ident_b")
         make_identity(nc, ident_f[:])
@@ -57,11 +52,11 @@ def tile_connectlayer_t_kernel(tc, x, connect_w, connect_mask, out):
         chunk_of = {}
         chunk_tiles = []
         first = 0
-        for n in LOADS:
-            xt = xo.tile([P, n * K], BF16, name="x%d" % first, offset=X_BASE + first * K * 2)
+        for n in CHUNKS:
+            xt = xo.tile([P, n * K], BF16, name="x%d" % first, offset=first * K * 2)
             chunk_tiles.append((xt, first, n))
             for t in range(n):
-                chunk_of[first + t] = (xt, first)
+                chunk_of[first + t] = (xt, first, n)
             first += n
 
         def load_w(dst, src, j):
@@ -70,7 +65,7 @@ def tile_connectlayer_t_kernel(tc, x, connect_w, connect_mask, out):
         def load_x(c):
             xt, f, n = chunk_tiles[c]
             nc.sync.dma_start(
-                out=xt[:].rearrange("p (t k) -> p t k", t=n), in_=x3[:, f : f + n, :]
+                out=xt[:], in_=x[f * P : (f + n) * P, :].rearrange("(p t) k -> p (t k)", t=n)
             )
 
         for j in range(WT):
@@ -80,10 +75,9 @@ def tile_connectlayer_t_kernel(tc, x, connect_w, connect_mask, out):
         load_x(1)
         load_w(mk, connect_mask, 1)
         load_w(mk, connect_mask, 2)
-        for c in range(2, len(LOADS)):
+        for c in range(2, len(CHUNKS)):
             load_x(c)
 
-        nmax = wpool.tile([P, WT], F32, name="nmax")
         rsum = wpool.tile([P, WT], F32, name="rsum")
         rinv = wpool.tile([P, WT], F32, name="rinv")
         ew = [wpool.tile([P, K], F32, name="ew%d" % j) for j in range(WT)]
@@ -92,12 +86,8 @@ def tile_connectlayer_t_kernel(tc, x, connect_w, connect_mask, out):
         wcod = wpool.tile([P, 2 * G], U32, name="wcod", align_bytes=64)
         wsca = wpool.tile([P, 2 * G], U8, name="wsca", align_bytes=64)
         for j in range(WT):
-            nc.vector.tensor_reduce(
-                out=nmax[:, j : j + 1], in_=cw[j][:], axis=AX.X, op=ALU.max, negate=True
-            )
-        for j in range(WT):
             nc.scalar.activation(
-                out=ew[j][:], in_=cw[j][:], func=ACT.Exp, bias=nmax[:, j : j + 1], scale=1.0
+                out=ew[j][:], in_=cw[j][:], func=ACT.Exp
             )
         for j in range(WT):
             nc.vector.scalar_tensor_tensor(
@@ -125,7 +115,7 @@ def tile_connectlayer_t_kernel(tc, x, connect_w, connect_mask, out):
         drained = set()
 
         def transposes(t):
-            xt, f = chunk_of[t]
+            xt, f, n = chunk_of[t]
             bank = tp.tile([P, 512], F32, name="tp%d" % t, tag="tp")
             xw = xt[:].bitcast(F32)
             for s in range(4):
@@ -179,7 +169,13 @@ def tile_connectlayer_t_kernel(tc, x, connect_w, connect_mask, out):
                 t, n = STORES[state["store"]]
                 if not all((t + k, part) in drained for k in range(n) for part in "ab"):
                     break
-                nc.sync.dma_start(out=out3[:, t : t + n, :], in_=out_view(t, n))
+                xt, f, m = chunk_of[t]
+                nc.sync.dma_start(
+                    out=out2[f * P : (f + m) * P, :].rearrange("(p t) c -> p t c", t=m)[
+                        :, t - f : t - f + n, :
+                    ],
+                    in_=out_view(t, n),
+                )
                 state["store"] += 1
 
         def drain(acc, t, n, c0, c1, on_vector):
@@ -195,39 +191,33 @@ def tile_connectlayer_t_kernel(tc, x, connect_w, connect_mask, out):
                 state["pending"] = None
                 stores()
 
-        def m_run(t):
-            flush_b()
-            accs = []
-            for h in range(2):
-                a = oa.tile([P, 512], F32, name="oa%d" % (t + 2 * h), tag="oa")
-                for k in range(2):
-                    mx_group(a[:, k * 256 : (k + 1) * 256], t + 2 * h + k, 0, 256)
-                accs.append(a)
-            if (t // 4) % 2 == 0:
+        def m_run(first_tile, count):
+            for t in range(first_tile, first_tile + count, 4):
+                flush_b()
+                accs = []
+                for h in range(2):
+                    a = oa.tile([P, 512], F32, name="oa%d" % (t + 2 * h), tag="oa")
+                    for k in range(2):
+                        mx_group(a[:, k * 256 : (k + 1) * 256], t + 2 * h + k, 0, 256)
+                    accs.append(a)
                 b = ob.tile([P, 512], F32, name="ob%d" % t, tag="ob")
-            else:
-                b = ex.tile([P, 512], F32, name="ex%d" % t, tag="ex")
-            for k in range(4):
-                mx_group(b[:, k * P : (k + 1) * P], t + k, 256, G)
-            for h in range(2):
-                drain(accs[h][:], t + 2 * h, 2, 0, 256, False)
-            state["pending"] = (b, t)
+                for k in range(4):
+                    mx_group(b[:, k * P : (k + 1) * P], t + k, 256, G)
+                for h in range(2):
+                    drain(accs[h][:], t + 2 * h, 2, 0, 256, False)
+                state["pending"] = (b, t)
 
-        def t_run(first_tile):
-            for k in range(4):
+        def t_run(first_tile, count, vector_tiles):
+            for k in range(count):
                 transposes(first_tile + k)
                 if k == 0:
                     flush_b()
-                regroup(first_tile + k, k == 2)
-            quantise(first_tile // 2)
-            quantise(first_tile // 2 + 1)
+                regroup(first_tile + k, k in vector_tiles)
+                if k % 2 == 1 and k >= 3:
+                    quantise((first_tile + k - 3) // 2)
+            quantise((first_tile + count - 2) // 2)
 
         wbank = []
-        junk = ex.tile([P, 512], F32, name="junk", tag="ex")
-
-        def idle_matmuls(n):
-            for i in range(n):
-                nc.tensor.matmul(out=junk[:], lhsT=zeros[:, 0:P], rhs=zeros[:], start=True, stop=True)
 
         def w_transposes(j):
             pool = oa if j < 2 else ob
@@ -256,19 +246,10 @@ def tile_connectlayer_t_kernel(tc, x, connect_w, connect_mask, out):
                     in_=gw[:, a * 4 : (a + P) * 4],
                 )
 
-        idle_matmuls(10)
-        transposes(0)
-        transposes(1)
-        idle_matmuls(2)
-        transposes(2)
-        transposes(3)
-        idle_matmuls(3)
-        w_transposes(0)
-        idle_matmuls(2)
-        w_transposes(1)
-        idle_matmuls(2)
-        w_transposes(2)
-        idle_matmuls(2)
+        for t in range(4):
+            transposes(t)
+        for j in range(WT):
+            w_transposes(j)
         regroup(0, True)
         regroup(1, True)
         w_regroup(0, True)
@@ -285,19 +266,21 @@ def tile_connectlayer_t_kernel(tc, x, connect_w, connect_mask, out):
         regroup(4, False)
         transposes(5)
         regroup(5, False)
-        idle_matmuls(2)
         quantise(2)
-        transposes(6)
-        regroup(6, False)
-        transposes(7)
-        regroup(7, True)
-        idle_matmuls(2)
-        quantise(3)
 
-        m_run(0)
-        for a in range(8, TILES, 4):
-            t_run(a)
-            m_run(a - 4)
+        m_run(0, 4)
+        t_run(6, 6, (2, 5))
+        m_run(4, 4)
+        if RUN == 4:
+            for a in range(12, TILES, 4):
+                t_run(a, 4, (2,))
+                m_run(a - 4, 4)
+        else:
+            for a in range(12, TILES - 4, 8):
+                t_run(a, 8, (2, 5, 7))
+                m_run(a - 4, 8)
+            t_run(TILES - 4, 4, (2,))
+            m_run(TILES - 8, 4)
 
         flush_b()
         t = TILES - 4

from contextlib import ExitStack

import concourse.mybir as mybir
from concourse.masks import make_identity

F32 = mybir.dt.float32
BF16 = mybir.dt.bfloat16
U32 = mybir.dt.uint32
U8 = mybir.dt.uint8
FP8X4 = mybir.dt.float8_e4m3fn_x4
ALU = mybir.AluOpType
ACT = mybir.ActivationFunctionType

P = 128
BATCH = 8192
K = 1024
G = 384
WT = G // P
TILES = BATCH // P
RUN = 4
CHUNKS = (2, 2, 4, 8, 8, 8, 8, 8, 8, 8)
OUT_BUFS = ((0, 4), (4, 4), (8, 8), (16, 8), (24, 8), (32, 8), (40, 8), (48, 8), (56, 4), (60, 4))
STORES = ((0, 2), (2, 2), (4, 4), (8, 8), (16, 8), (24, 8), (32, 8), (40, 8), (48, 8), (56, 4), (60, 2), (62, 1), (63, 1))

FLOPS = 2 * BATCH * K * G


def tile_connectlayer_t_kernel(tc, x, connect_w, connect_mask, out):
    nc = tc.nc
    out2 = out.rearrange("b d s -> b (d s)")
    with ExitStack() as ctx:
        const = ctx.enter_context(tc.tile_pool(name="const", bufs=1))
        wpool = ctx.enter_context(tc.tile_pool(name="wpool", bufs=1))
        xo = ctx.enter_context(tc.tile_pool(name="xo", bufs=1))
        grp = ctx.enter_context(tc.tile_pool(name="grp", bufs=4))
        cod = ctx.enter_context(tc.tile_pool(name="cod", bufs=6))
        tp = ctx.enter_context(tc.psum_pool(name="tp", bufs=5))
        oa = ctx.enter_context(tc.psum_pool(name="oa", bufs=2))
        ob = ctx.enter_context(tc.psum_pool(name="ob", bufs=1))
        ctx.enter_context(tc.manual_schedule())

        ident_f = const.tile([P, P], F32, name="ident_f")
        ident_b = const.tile([P, P], BF16, name="ident_b")
        make_identity(nc, ident_f[:])
        make_identity(nc, ident_b[:])
        warm = const.tile([P, 2], F32, name="warm")
        nc.vector.memset(warm[:, 0:1], 0.0)
        nc.scalar.activation(out=warm[:, 1:2], in_=warm[:, 0:1], func=ACT.Exp)

        cw = [wpool.tile([P, K], BF16, name="cw%d" % j) for j in range(WT)]
        mk = [wpool.tile([P, K], BF16, name="mk%d" % j) for j in range(WT)]
        chunk_of = {}
        chunk_tiles = []
        first = 0
        for n in CHUNKS:
            xt = xo.tile([P, n * K], BF16, name="x%d" % first, offset=first * K * 2)
            chunk_tiles.append((xt, first, n))
            for t in range(n):
                chunk_of[first + t] = (xt, first, n)
            first += n

        def load_w(dst, src, j):
            nc.sync.dma_start(out=dst[j][:], in_=src[j * P : (j + 1) * P, :])

        def load_x(c):
            xt, f, n = chunk_tiles[c]
            nc.sync.dma_start(
                out=xt[:], in_=x[f * P : (f + n) * P, :].rearrange("(p t) k -> p (t k)", t=n)
            )

        for j in range(WT):
            load_w(cw, connect_w, j)
        load_x(0)
        load_w(mk, connect_mask, 0)
        load_x(1)
        load_w(mk, connect_mask, 1)
        load_w(mk, connect_mask, 2)
        for c in range(2, len(CHUNKS)):
            load_x(c)

        rsum = wpool.tile([P, WT], F32, name="rsum")
        rinv = wpool.tile([P, WT], F32, name="rinv")
        ew = [wpool.tile([P, K], F32, name="ew%d" % j) for j in range(WT)]
        wb = [wpool.tile([P, K], BF16, name="wb%d" % j) for j in range(WT)]
        gw = wpool.tile([P, 2 * G * 4], BF16, name="gw", align_bytes=64)
        wcod = wpool.tile([P, 2 * G], U32, name="wcod", align_bytes=64)
        wsca = wpool.tile([P, 2 * G], U8, name="wsca", align_bytes=64)
        for j in range(WT):
            nc.scalar.activation(
                out=ew[j][:], in_=cw[j][:], func=ACT.Exp
            )
        for j in range(WT):
            nc.vector.scalar_tensor_tensor(
                out=ew[j][:],
                in0=ew[j][:],
                scalar=1.0,
                in1=mk[j][:],
                op0=ALU.mult,
                op1=ALU.mult,
                accum_out=rsum[:, j : j + 1],
            )
            nc.vector.reciprocal(out=rinv[:, j : j + 1], in_=rsum[:, j : j + 1])
            nc.scalar.activation(
                out=wb[j][:].rearrange("p (a e q) -> p a e q", a=4, e=2, q=P),
                in_=ew[j][:].rearrange("p (a q e) -> p a e q", a=4, q=P, e=2),
                func=ACT.Copy,
                scale=rinv[:, j : j + 1],
            )

        banks = {}
        halves = {}
        codes = {}
        out_of = {}
        state = {"pending": None, "store": 0}
        drained = set()

        def transposes(t):
            xt, f, n = chunk_of[t]
            bank = tp.tile([P, 512], F32, name="tp%d" % t, tag="tp")
            xw = xt[:].bitcast(F32)
            for s in range(4):
                a = (t - f) * 512 + s * P
                nc.tensor.transpose(bank[:, s * P : (s + 1) * P], xw[:, a : a + P], ident_f[:])
            banks[t] = bank

        def regroup(t, on_vector):
            q = t // 2
            if q not in halves:
                halves[q] = grp.tile([P, 2048], BF16, name="g%d" % q, tag="g", align_bytes=64)
            dst = halves[q][:].bitcast(F32)[:, (t % 2) * 512 : (t % 2 + 1) * 512]
            copy = nc.vector.tensor_copy if on_vector else nc.scalar.copy
            copy(
                out=dst.rearrange("p (g b u) -> p g b u", g=2, b=P, u=2),
                in_=banks[t][:].rearrange("p (g u b) -> p g b u", g=2, u=2, b=P),
            )

        def quantise(q):
            c = cod.tile([P, 512], U32, name="c%d" % q, tag="c", align_bytes=64)
            s = cod.tile([P, 512], U8, name="s%d" % q, tag="s", align_bytes=64)
            nc.vector.quantize_mx(out=c[:].bitcast(FP8X4), scales=s[:], in_=halves[q][:])
            codes[q] = (c, s)

        def mx_group(dst, t, c0, c1):
            c, s = codes[t // 2]
            for g in range(2):
                a = ((t % 2) * 2 + g) * P
                nc.tensor.matmul_mx(
                    out=dst,
                    lhsT=c[:, a : a + P].bitcast(FP8X4),
                    lhsT_scale=s[:, a : a + P],
                    rhs=wcod[:, g * G + c0 : g * G + c1].bitcast(FP8X4),
                    rhs_scale=wsca[:, g * G + c0 : g * G + c1],
                    start=(g == 0),
                    stop=(g == 1),
                )

        def out_view(t, n):
            if t not in out_of:
                for f, m in OUT_BUFS:
                    if f <= t < f + m:
                        o = xo.tile([P, m * G], F32, name="o%d" % f, offset=f * G * 4)
                        for k in range(m):
                            out_of[f + k] = (o, f, m)
            o, f, m = out_of[t]
            return o[:].rearrange("p (t c) -> p t c", t=m)[:, t - f : t - f + n, :]

        def stores():
            while state["store"] < len(STORES):
                t, n = STORES[state["store"]]
                if not all((t + k, part) in drained for k in range(n) for part in "ab"):
                    break
                xt, f, m = chunk_of[t]
                nc.sync.dma_start(
                    out=out2[f * P : (f + m) * P, :].rearrange("(p t) c -> p t c", t=m)[
                        :, t - f : t - f + n, :
                    ],
                    in_=out_view(t, n),
                )
                state["store"] += 1

        def drain(acc, t, n, c0, c1, on_vector):
            copy = nc.vector.tensor_copy if on_vector else nc.scalar.copy
            copy(out=out_view(t, n)[:, :, c0:c1], in_=acc.rearrange("p (t c) -> p t c", t=n))
            for k in range(n):
                drained.add((t + k, "a" if c0 == 0 else "b"))

        def flush_b():
            if state["pending"] is not None:
                acc, t = state["pending"]
                drain(acc[:], t, 4, 256, G, True)
                state["pending"] = None
                stores()

        def m_run(first_tile, count):
            for t in range(first_tile, first_tile + count, 4):
                flush_b()
                accs = []
                for h in range(2):
                    a = oa.tile([P, 512], F32, name="oa%d" % (t + 2 * h), tag="oa")
                    for k in range(2):
                        mx_group(a[:, k * 256 : (k + 1) * 256], t + 2 * h + k, 0, 256)
                    accs.append(a)
                b = ob.tile([P, 512], F32, name="ob%d" % t, tag="ob")
                for k in range(4):
                    mx_group(b[:, k * P : (k + 1) * P], t + k, 256, G)
                for h in range(2):
                    drain(accs[h][:], t + 2 * h, 2, 0, 256, False)
                state["pending"] = (b, t)

        def t_run(first_tile, count, vector_tiles):
            for k in range(count):
                transposes(first_tile + k)
                if k == 0:
                    flush_b()
                regroup(first_tile + k, k in vector_tiles)
                if k % 2 == 1 and k >= 3:
                    quantise((first_tile + k - 3) // 2)
            quantise((first_tile + count - 2) // 2)

        wbank = []

        def w_transposes(j):
            pool = oa if j < 2 else ob
            b = pool.tile([P, K], BF16, name="wt%d" % j, tag="oa" if j < 2 else "ob")
            for s in range(8):
                nc.tensor.transpose(
                    b[:, s * P : (s + 1) * P], wb[j][:, s * P : (s + 1) * P], ident_b[:]
                )
            wbank.append(b)

        def w_regroup(j, on_vector):
            copy = nc.vector.tensor_copy if on_vector else nc.scalar.copy
            copy(
                out=gw[:].rearrange("p (g c t) -> p g c t", g=2, c=G, t=4)[
                    :, :, j * P : (j + 1) * P, :
                ],
                in_=wbank[j][:].rearrange("p (g t c) -> p g c t", g=2, t=4, c=P),
            )

        def w_quantise(j):
            for g in range(2):
                a = g * G + j * P
                nc.vector.quantize_mx(
                    out=wcod[:, a : a + P].bitcast(FP8X4),
                    scales=wsca[:, a : a + P],
                    in_=gw[:, a * 4 : (a + P) * 4],
                )

        for t in range(4):
            transposes(t)
        for j in range(WT):
            w_transposes(j)
        regroup(0, True)
        regroup(1, True)
        w_regroup(0, True)
        w_regroup(1, False)
        quantise(0)
        w_quantise(0)
        w_quantise(1)
        regroup(2, False)
        regroup(3, False)
        w_regroup(2, False)
        quantise(1)
        w_quantise(2)
        transposes(4)
        regroup(4, False)
        transposes(5)
        regroup(5, False)
        quantise(2)

        m_run(0, 4)
        t_run(6, 6, (2, 5))
        m_run(4, 4)
        if RUN == 4:
            for a in range(12, TILES, 4):
                t_run(a, 4, (2,))
                m_run(a - 4, 4)
        else:
            for a in range(12, TILES - 4, 8):
                t_run(a, 8, (2, 5, 7))
                m_run(a - 4, 8)
            t_run(TILES - 4, 4, (2,))
            m_run(TILES - 8, 4)

        flush_b()
        t = TILES - 4
        b = tp.tile([P, 512], F32, name="last_b", tag="tp")
        for k in range(4):
            mx_group(b[:, k * P : (k + 1) * P], t + k, 256, G)
        drain(b[:], t, 4, 256, G, True)
        a = oa.tile([P, 512], F32, name="last_a", tag="oa")
        for k in range(2):
            mx_group(a[:, k * 256 : (k + 1) * 256], t + k, 0, 256)
        drain(a[:], t, 2, 0, 256, False)
        stores()
        a2 = oa.tile([P, 256], F32, name="last_a2", tag="oa")
        mx_group(a2[:], t + 2, 0, 256)
        drain(a2[:], t + 2, 1, 0, 256, False)
        stores()
        a3 = tp.tile([P, 256], F32, name="last_a3", tag="tp")
        mx_group(a3[:], t + 3, 0, 256)
        drain(a3[:], t + 3, 1, 0, 256, True)
        stores()
